import numpy as np
import ml_dtypes


def mxq(x, axis, fmt="e4m3"):
    dtype, down = {"e4m3": (ml_dtypes.float8_e4m3fn, 7), "e5m2": (ml_dtypes.float8_e5m2, 14)}[fmt]
    v = np.moveaxis(np.asarray(x, np.float32).astype(ml_dtypes.bfloat16).astype(np.float64), axis, -1)
    blocks = v.reshape(v.shape[:-1] + (-1, 32))
    amax = np.abs(blocks).max(-1, keepdims=True)
    byte = np.maximum(np.where(amax > 0, np.frexp(amax)[1] - 1 + 127, 0) - down, 1)
    scale = np.exp2(byte - 127.0)
    codes = (blocks / scale).astype(np.float32).astype(dtype).astype(np.float64)
    return np.moveaxis((codes * scale).reshape(v.shape), -1, axis)


WIDE = False


def mx_kscale(k):
    if not WIDE:
        return np.ones(k)
    levels = np.array([10, -10, 5, -5, 0])
    if k % 512:
        return np.exp2(np.random.permutation(np.resize(levels, k // 32))).repeat(32)
    a = np.empty((k // 512, 16))
    for p in range(k // 512):
        a[p, :8] = np.random.permutation(np.resize(levels, 8))
        for g in range(8):
            far = levels[np.abs(levels - a[p, g]) >= 10]
            a[p, g + 8] = far[np.random.randint(len(far))]
    return np.exp2(a.ravel()).repeat(32)


BF16 = ml_dtypes.bfloat16


def bf(x):
    return np.asarray(x, np.float32).astype(BF16)


def f64(x):
    return np.asarray(x).astype(np.float64)


B, N, D, F, C, L = 128, 512, 1024, 256, 128, 28
EPS = 1e-12


def l2norm(x):
    n = np.sqrt(np.sum(x * x, axis=1, keepdims=True))
    return x / np.maximum(n, EPS)


def setup_inputs():
    s = mx_kscale(D)
    return {"features": bf(np.random.standard_normal((B, D)) * s),
            "ex_features": bf(np.random.standard_normal((N, D)) * s),
            "g_weight": bf(np.random.standard_normal((F, D)) / np.sqrt(D) / s)}


def reference(features, ex_features, g_weight):
    gq = mxq(f64(g_weight), 1, "e4m3")
    f = mxq(f64(features), 1, "e4m3") @ gq.T
    exf = mxq(f64(ex_features), 1, "e4m3") @ gq.T
    return l2norm(f), l2norm(exf)

@@ -1,0 +1,164 @@
+from contextlib import ExitStack
+
+import concourse.mybir as mybir
+from concourse.masks import make_identity
+
+F32 = mybir.dt.float32
+BF16 = mybir.dt.bfloat16
+U32 = mybir.dt.uint32
+U8 = mybir.dt.uint8
+FP8X4 = mybir.dt.float8_e4m3fn_x4
+ACT = mybir.ActivationFunctionType
+ALU = mybir.AluOpType
+
+P = 128
+PACK = 4
+K = 1024
+K_PASS = P * PACK
+PASSES = K // K_PASS
+HALVES = 2
+BLOCKS = PASSES * HALVES
+F = 256
+G_TILES = F // P
+EX_TILES = 4
+X_TILES = 1 + EX_TILES
+EPS = 1e-12
+WARM_MATMULS = 4
+IDLE_N = 64
+
+FLOPS = 2 * (X_TILES * P) * F * K
+
+
+def tile_minerva_old_pa_s_kernel(tc, features, ex_features, g_weight, out_0, out_1):
+    nc = tc.nc
+    with ExitStack() as ctx:
+        const = ctx.enter_context(tc.tile_pool(name="const", bufs=1))
+        raw_pool = ctx.enter_context(tc.tile_pool(name="raw", bufs=G_TILES + X_TILES))
+        x_pool = ctx.enter_context(tc.tile_pool(name="x", bufs=X_TILES))
+        banks = ctx.enter_context(tc.psum_pool(name="banks", bufs=7))
+        idle_pool = ctx.enter_context(tc.psum_pool(name="idle", bufs=1))
+        ctx.enter_context(tc.manual_schedule())
+
+        g_rows = g_weight.rearrange("(j p) k -> j p k", p=P)
+        ex_rows = ex_features.rearrange("(p t) k -> t p k", t=EX_TILES)
+        ex_out = out_1.rearrange("(p t) n -> t p n", t=EX_TILES)
+        x_rows = [features] + [ex_rows[t] for t in range(EX_TILES)]
+        x_out = [out_0] + [ex_out[t] for t in range(EX_TILES)]
+
+        def load(rows):
+            raw = raw_pool.tile([P, K], BF16)
+            nc.sync.dma_start(out=raw[:], in_=rows)
+            return raw
+
+        g_raw = [load(g_rows[j]) for j in range(G_TILES)]
+        x_raw = [load(x_rows[i]) for i in range(X_TILES)]
+
+        ident = const.tile([P, P], F32)
+        make_identity(nc, ident[:])
+
+        ones = const.tile([P, P], F32)
+        nc.vector.memset(ones[:], 1.0)
+        idle_bank = idle_pool.tile([P, P], F32)
+        for w in range(WARM_MATMULS):
+            nc.tensor.matmul(out=idle_bank[:], lhsT=ones[:], rhs=ones[:], start=True, stop=True)
+
+        also_one = const.tile([P, 1], F32)
+        nc.scalar.activation(out=also_one[:], in_=ones[:, :1], func=ACT.Abs_reciprocal_sqrt)
+
+        def stay_busy():
+            nc.tensor.matmul(
+                out=idle_bank[:, :IDLE_N], lhsT=ones[:], rhs=ones[:, :IDLE_N], start=True, stop=True
+            )
+
+        def transpose_and_regroup(copy, raw, grouped_words):
+            words = raw[:].bitcast(F32)
+            bank = banks.tile([P, BLOCKS, P], F32, tag="bank")
+            stay_busy()
+            for b in range(BLOCKS):
+                g, u = divmod(b, HALVES)
+                first = g * HALVES * P
+                nc.tensor.transpose(
+                    bank[:, b, :], words[:, first + u : first + HALVES * P : HALVES], ident[:]
+                )
+            copy(out=grouped_words, in_=bank[:].rearrange("p (g u) r -> p g r u", u=HALVES))
+
+        g_grouped = const.tile([P, PASSES * F * PACK], BF16, align_bytes=64)
+        g_codes = const.tile([P, PASSES * F], U32, align_bytes=64)
+        g_scales = const.tile([P, PASSES * F], U8, align_bytes=64)
+        g_words = g_grouped[:].bitcast(F32).rearrange("p (g n u) -> p g n u", g=PASSES, u=HALVES)
+        for j in range(G_TILES):
+            transpose_and_regroup(nc.vector.tensor_copy, g_raw[j], g_words[:, :, j * P : (j + 1) * P, :])
+
+        x_grouped = {}
+        x_codes = {}
+        x_scales = {}
+
+        def bring_in(i):
+            grouped = x_pool.tile([P, PASSES * P * PACK], BF16, align_bytes=64)
+            transpose_and_regroup(
+                nc.scalar.copy,
+                x_raw[i],
+                grouped[:].bitcast(F32).rearrange("p (g r u) -> p g r u", g=PASSES, u=HALVES),
+            )
+            x_grouped[i] = grouped
+
+        def quantise(i):
+            codes = x_pool.tile([P, PASSES * P], U32, align_bytes=64)
+            scales = x_pool.tile([P, PASSES * P], U8, align_bytes=64)
+            nc.vector.quantize_mx(
+                out=codes[:].bitcast(FP8X4), scales=scales[:], in_=x_grouped[i][:]
+            )
+            x_codes[i] = codes
+            x_scales[i] = scales
+
+        def project(i):
+            acc = banks.tile([P, F], F32, tag="bank")
+            for g in range(PASSES):
+                nc.tensor.matmul_mx(
+                    out=acc[:],
+                    lhsT=x_codes[i][:, g * P : (g + 1) * P].bitcast(FP8X4),
+                    lhsT_scale=x_scales[i][:, g * P : (g + 1) * P],
+                    rhs=g_codes[:, g * F : (g + 1) * F].bitcast(FP8X4),
+                    rhs_scale=g_scales[:, g * F : (g + 1) * F],
+                    start=(g == 0),
+                    stop=(g == PASSES - 1),
+                )
+            return acc
+
+        def sum_of_squares(acc):
+            squares = x_pool.tile([P, F], F32)
+            sum_sq = x_pool.tile([P, 1], F32)
+            nc.scalar.activation(out=squares[:], in_=acc[:], func=ACT.Square, accum_out=sum_sq[:])
+            return sum_sq
+
+        def scale_and_store(i, acc, sum_sq):
+            inv_root = x_pool.tile([P, 1], F32)
+            nc.scalar.activation(out=inv_root[:], in_=sum_sq[:], func=ACT.Abs_reciprocal_sqrt)
+            unit = x_pool.tile([P, F], F32)
+            nc.vector.scalar_tensor_tensor(
+                out=unit[:],
+                in0=inv_root[:].to_broadcast([P, F]),
+                scalar=1.0 / EPS,
+                in1=acc[:],
+                op0=ALU.min,
+                op1=ALU.mult,
+            )
+            nc.sync.dma_start(out=x_out[i], in_=unit[:])
+
+        for i in range(X_TILES):
+            bring_in(i)
+            if i == 0:
+                nc.vector.quantize_mx(
+                    out=g_codes[:].bitcast(FP8X4), scales=g_scales[:], in_=g_grouped[:]
+                )
+            else:
+                quantise(i - 1)
+        quantise(X_TILES - 1)
+        accs = {}
+        sums = {}
+        for i in range(X_TILES + 1):
+            if i < X_TILES:
+                accs[i] = project(i)
+                sums[i] = sum_of_squares(accs[i])
+            if i > 0:
+                scale_and_store(i - 1, accs[i - 1], sums[i - 1])

@@ -17,7 +17,6 @@ K = 1024
 K_PASS = P * PACK
 PASSES = K // K_PASS
 HALVES = 2
-BLOCKS = PASSES * HALVES
 F = 256
 G_TILES = F // P
 EX_TILES = 4
@@ -25,6 +24,7 @@ X_TILES = 1 + EX_TILES
 EPS = 1e-12
 WARM_MATMULS = 4
 IDLE_N = 64
+IDLE_EVERY = 2
 
 FLOPS = 2 * (X_TILES * P) * F * K
 
@@ -70,24 +70,29 @@ def tile_minerva_old_pa_s_kernel(tc, features, ex_features, g_weight, out_0, out
                 out=idle_bank[:, :IDLE_N], lhsT=ones[:], rhs=ones[:, :IDLE_N], start=True, stop=True
             )
 
-        def transpose_and_regroup(copy, raw, grouped_words):
-            words = raw[:].bitcast(F32)
-            bank = banks.tile([P, BLOCKS, P], F32, tag="bank")
-            stay_busy()
-            for b in range(BLOCKS):
-                g, u = divmod(b, HALVES)
-                first = g * HALVES * P
-                nc.tensor.transpose(
-                    bank[:, b, :], words[:, first + u : first + HALVES * P : HALVES], ident[:]
+        def transpose_and_regroup(copies, raw, grouped_words):
+            words = raw[:].bitcast(F32).rearrange("r (g p u) -> r g u p", g=PASSES, u=HALVES)
+            for copy, passes in copies:
+                bank = banks.tile([P, passes.stop - passes.start, HALVES, P], F32, tag="bank")
+                for g in range(passes.start, passes.stop):
+                    for u in range(HALVES):
+                        nc.tensor.transpose(
+                            bank[:, g - passes.start, u, :], words[:, g, u, :], ident[:]
+                        )
+                copy(
+                    out=grouped_words[:, passes], in_=bank[:].rearrange("p g u r -> p g r u")
                 )
-            copy(out=grouped_words, in_=bank[:].rearrange("p (g u) r -> p g r u", u=HALVES))
 
         g_grouped = const.tile([P, PASSES * F * PACK], BF16, align_bytes=64)
         g_codes = const.tile([P, PASSES * F], U32, align_bytes=64)
         g_scales = const.tile([P, PASSES * F], U8, align_bytes=64)
         g_words = g_grouped[:].bitcast(F32).rearrange("p (g n u) -> p g n u", g=PASSES, u=HALVES)
-        for j in range(G_TILES):
-            transpose_and_regroup(nc.vector.tensor_copy, g_raw[j], g_words[:, :, j * P : (j + 1) * P, :])
+        whole = slice(0, PASSES)
+        for j, copy in enumerate([nc.vector.tensor_copy, nc.scalar.copy]):
+            grouped_words = g_words[:, :, j * P : (j + 1) * P, :]
+            if j % IDLE_EVERY:
+                stay_busy()
+            transpose_and_regroup([(copy, whole)], g_raw[j], grouped_words)
 
         x_grouped = {}
         x_codes = {}
@@ -95,8 +100,12 @@ def tile_minerva_old_pa_s_kernel(tc, features, ex_features, g_weight, out_0, out
 
         def bring_in(i):
             grouped = x_pool.tile([P, PASSES * P * PACK], BF16, align_bytes=64)
+            if i < X_TILES - 1:
+                copies = [(nc.scalar.copy, whole)]
+            else:
+                copies = [(nc.scalar.copy, slice(0, 1)), (nc.vector.tensor_copy, slice(1, 2))]
             transpose_and_regroup(
-                nc.scalar.copy,
+                copies,
                 x_raw[i],
                 grouped[:].bitcast(F32).rearrange("p (g r u) -> p g r u", g=PASSES, u=HALVES),
             )
@@ -146,6 +155,8 @@ def tile_minerva_old_pa_s_kernel(tc, features, ex_features, g_weight, out_0, out
             nc.sync.dma_start(out=x_out[i], in_=unit[:])
 
         for i in range(X_TILES):
+            if (G_TILES + i) % IDLE_EVERY:
+                stay_busy()
             bring_in(i)
             if i == 0:
                 nc.vector.quantize_mx(

@@ -23,7 +23,7 @@ EX_TILES = 4
 X_TILES = 1 + EX_TILES
 EPS = 1e-12
 WARM_MATMULS = 4
-IDLE_N = 64
+IDLE_N = 128
 IDLE_EVERY = 2
 
 FLOPS = 2 * (X_TILES * P) * F * K

@@ -45,12 +45,14 @@ def tile_minerva_old_pa_s_kernel(tc, features, ex_features, g_weight, out_0, out
         x_rows = [features] + [ex_rows[t] for t in range(EX_TILES)]
         x_out = [out_0] + [ex_out[t] for t in range(EX_TILES)]
 
-        def load(rows):
+        def load(rows, pieces=1):
             raw = raw_pool.tile([P, K], BF16)
-            nc.sync.dma_start(out=raw[:], in_=rows)
+            width = K // pieces
+            for c in range(0, K, width):
+                nc.sync.dma_start(out=raw[:, c : c + width], in_=rows[:, c : c + width])
             return raw
 
-        g_raw = [load(g_rows[j]) for j in range(G_TILES)]
+        g_raw = [load(g_rows[0], PASSES), load(g_rows[1])]
         x_raw = [load(x_rows[i]) for i in range(X_TILES)]
 
         ident = const.tile([P, P], F32)

from contextlib import ExitStack

import concourse.mybir as mybir
from concourse.masks import make_identity

F32 = mybir.dt.float32
BF16 = mybir.dt.bfloat16
U32 = mybir.dt.uint32
U8 = mybir.dt.uint8
FP8X4 = mybir.dt.float8_e4m3fn_x4
ACT = mybir.ActivationFunctionType
ALU = mybir.AluOpType

P = 128
PACK = 4
K = 1024
K_PASS = P * PACK
PASSES = K // K_PASS
HALVES = 2
F = 256
G_TILES = F // P
EX_TILES = 4
X_TILES = 1 + EX_TILES
EPS = 1e-12
WARM_MATMULS = 4
IDLE_N = 128
IDLE_EVERY = 2

FLOPS = 2 * (X_TILES * P) * F * K


def tile_minerva_old_pa_s_kernel(tc, features, ex_features, g_weight, out_0, out_1):
    nc = tc.nc
    with ExitStack() as ctx:
        const = ctx.enter_context(tc.tile_pool(name="const", bufs=1))
        raw_pool = ctx.enter_context(tc.tile_pool(name="raw", bufs=G_TILES + X_TILES))
        x_pool = ctx.enter_context(tc.tile_pool(name="x", bufs=X_TILES))
        banks = ctx.enter_context(tc.psum_pool(name="banks", bufs=7))
        idle_pool = ctx.enter_context(tc.psum_pool(name="idle", bufs=1))
        ctx.enter_context(tc.manual_schedule())

        g_rows = g_weight.rearrange("(j p) k -> j p k", p=P)
        ex_rows = ex_features.rearrange("(p t) k -> t p k", t=EX_TILES)
        ex_out = out_1.rearrange("(p t) n -> t p n", t=EX_TILES)
        x_rows = [features] + [ex_rows[t] for t in range(EX_TILES)]
        x_out = [out_0] + [ex_out[t] for t in range(EX_TILES)]

        def load(rows, pieces=1):
            raw = raw_pool.tile([P, K], BF16)
            width = K // pieces
            for c in range(0, K, width):
                nc.sync.dma_start(out=raw[:, c : c + width], in_=rows[:, c : c + width])
            return raw

        g_raw = [load(g_rows[0], PASSES), load(g_rows[1])]
        x_raw = [load(x_rows[i]) for i in range(X_TILES)]

        ident = const.tile([P, P], F32)
        make_identity(nc, ident[:])

        ones = const.tile([P, P], F32)
        nc.vector.memset(ones[:], 1.0)
        idle_bank = idle_pool.tile([P, P], F32)
        for w in range(WARM_MATMULS):
            nc.tensor.matmul(out=idle_bank[:], lhsT=ones[:], rhs=ones[:], start=True, stop=True)

        also_one = const.tile([P, 1], F32)
        nc.scalar.activation(out=also_one[:], in_=ones[:, :1], func=ACT.Abs_reciprocal_sqrt)

        def stay_busy():
            nc.tensor.matmul(
                out=idle_bank[:, :IDLE_N], lhsT=ones[:], rhs=ones[:, :IDLE_N], start=True, stop=True
            )

        def transpose_and_regroup(copies, raw, grouped_words):
            words = raw[:].bitcast(F32).rearrange("r (g p u) -> r g u p", g=PASSES, u=HALVES)
            for copy, passes in copies:
                bank = banks.tile([P, passes.stop - passes.start, HALVES, P], F32, tag="bank")
                for g in range(passes.start, passes.stop):
                    for u in range(HALVES):
                        nc.tensor.transpose(
                            bank[:, g - passes.start, u, :], words[:, g, u, :], ident[:]
                        )
                copy(
                    out=grouped_words[:, passes], in_=bank[:].rearrange("p g u r -> p g r u")
                )

        g_grouped = const.tile([P, PASSES * F * PACK], BF16, align_bytes=64)
        g_codes = const.tile([P, PASSES * F], U32, align_bytes=64)
        g_scales = const.tile([P, PASSES * F], U8, align_bytes=64)
        g_words = g_grouped[:].bitcast(F32).rearrange("p (g n u) -> p g n u", g=PASSES, u=HALVES)
        whole = slice(0, PASSES)
        for j, copy in enumerate([nc.vector.tensor_copy, nc.scalar.copy]):
            grouped_words = g_words[:, :, j * P : (j + 1) * P, :]
            if j % IDLE_EVERY:
                stay_busy()
            transpose_and_regroup([(copy, whole)], g_raw[j], grouped_words)

        x_grouped = {}
        x_codes = {}
        x_scales = {}

        def bring_in(i):
            grouped = x_pool.tile([P, PASSES * P * PACK], BF16, align_bytes=64)
            if i < X_TILES - 1:
                copies = [(nc.scalar.copy, whole)]
            else:
                copies = [(nc.scalar.copy, slice(0, 1)), (nc.vector.tensor_copy, slice(1, 2))]
            transpose_and_regroup(
                copies,
                x_raw[i],
                grouped[:].bitcast(F32).rearrange("p (g r u) -> p g r u", g=PASSES, u=HALVES),
            )
            x_grouped[i] = grouped

        def quantise(i):
            codes = x_pool.tile([P, PASSES * P], U32, align_bytes=64)
            scales = x_pool.tile([P, PASSES * P], U8, align_bytes=64)
            nc.vector.quantize_mx(
                out=codes[:].bitcast(FP8X4), scales=scales[:], in_=x_grouped[i][:]
            )
            x_codes[i] = codes
            x_scales[i] = scales

        def project(i):
            acc = banks.tile([P, F], F32, tag="bank")
            for g in range(PASSES):
                nc.tensor.matmul_mx(
                    out=acc[:],
                    lhsT=x_codes[i][:, g * P : (g + 1) * P].bitcast(FP8X4),
                    lhsT_scale=x_scales[i][:, g * P : (g + 1) * P],
                    rhs=g_codes[:, g * F : (g + 1) * F].bitcast(FP8X4),
                    rhs_scale=g_scales[:, g * F : (g + 1) * F],
                    start=(g == 0),
                    stop=(g == PASSES - 1),
                )
            return acc

        def sum_of_squares(acc):
            squares = x_pool.tile([P, F], F32)
            sum_sq = x_pool.tile([P, 1], F32)
            nc.scalar.activation(out=squares[:], in_=acc[:], func=ACT.Square, accum_out=sum_sq[:])
            return sum_sq

        def scale_and_store(i, acc, sum_sq):
            inv_root = x_pool.tile([P, 1], F32)
            nc.scalar.activation(out=inv_root[:], in_=sum_sq[:], func=ACT.Abs_reciprocal_sqrt)
            unit = x_pool.tile([P, F], F32)
            nc.vector.scalar_tensor_tensor(
                out=unit[:],
                in0=inv_root[:].to_broadcast([P, F]),
                scalar=1.0 / EPS,
                in1=acc[:],
                op0=ALU.min,
                op1=ALU.mult,
            )
            nc.sync.dma_start(out=x_out[i], in_=unit[:])

        for i in range(X_TILES):
            if (G_TILES + i) % IDLE_EVERY:
                stay_busy()
            bring_in(i)
            if i == 0:
                nc.vector.quantize_mx(
                    out=g_codes[:].bitcast(FP8X4), scales=g_scales[:], in_=g_grouped[:]
                )
            else:
                quantise(i - 1)
        quantise(X_TILES - 1)
        accs = {}
        sums = {}
        for i in range(X_TILES + 1):
            if i < X_TILES:
                accs[i] = project(i)
                sums[i] = sum_of_squares(accs[i])
            if i > 0:
                scale_and_store(i - 1, accs[i - 1], sums[i - 1])
